import numpy as np
import ml_dtypes


def mxq(x, axis, fmt="e4m3"):
    dtype, down = {"e4m3": (ml_dtypes.float8_e4m3fn, 7), "e5m2": (ml_dtypes.float8_e5m2, 14)}[fmt]
    v = np.moveaxis(np.asarray(x, np.float32).astype(ml_dtypes.bfloat16).astype(np.float64), axis, -1)
    blocks = v.reshape(v.shape[:-1] + (-1, 32))
    amax = np.abs(blocks).max(-1, keepdims=True)
    byte = np.maximum(np.where(amax > 0, np.frexp(amax)[1] - 1 + 127, 0) - down, 1)
    scale = np.exp2(byte - 127.0)
    codes = (blocks / scale).astype(np.float32).astype(dtype).astype(np.float64)
    return np.moveaxis((codes * scale).reshape(v.shape), -1, axis)


WIDE = False


def mx_kscale(k):
    if not WIDE:
        return np.ones(k)
    levels = np.array([30, -30])
    if k % 512:
        return np.exp2(np.random.permutation(np.resize(levels, k // 32))).repeat(32)
    a = np.empty((k // 512, 16))
    for p in range(k // 512):
        a[p, :8] = np.random.permutation(np.resize(levels, 8))
        for g in range(8):
            far = levels[np.abs(levels - a[p, g]) >= 10]
            a[p, g + 8] = far[np.random.randint(len(far))]
    return np.exp2(a.ravel()).repeat(32)


BF16 = ml_dtypes.bfloat16


def bf(x):
    return np.asarray(x, np.float32).astype(BF16)


def f64(x):
    return np.asarray(x).astype(np.float64)


DIM, H, HD, KV, B, S = 1024, 8, 128, 2, 4, 512
T = B * S
THETA = 10000.0


def apply_rope(t, cos, sin):
    tr = t.reshape(t.shape[0], t.shape[1], -1, 2)
    t1, t2 = tr[..., 0], tr[..., 1]
    c = cos[:, None, :]
    s = sin[:, None, :]
    o1 = t1 * c - t2 * s
    o2 = t1 * s + t2 * c
    return np.stack([o1, o2], axis=-1).reshape(t.shape)


def setup_inputs():
    s = mx_kscale(DIM)
    inv_freq = 1.0 / THETA ** (np.arange(0, HD, 2) / HD)
    pos = np.tile(np.arange(S), B)
    angles = pos[:, None] * inv_freq[None, :]
    return {"x": bf(np.random.standard_normal((T, DIM)) * s),
            "freqs_cos": bf(np.cos(angles)),
            "freqs_sin": bf(np.sin(angles)),
            "wq": bf(np.random.standard_normal((DIM, H * HD)) * 1.4 / np.sqrt(DIM) / s[:, None]),
            "wk": bf(np.random.standard_normal((DIM, KV * HD)) * 1.4 / np.sqrt(DIM) / s[:, None]),
            "wv": bf(np.random.standard_normal((DIM, KV * HD)) / np.sqrt(DIM) / s[:, None])}


def reference(x, freqs_cos, freqs_sin, wq, wk, wv):
    xm = mxq(f64(x), 1, "e5m2")
    q = (xm @ mxq(f64(wq), 0, "e4m3")).reshape(T, H, HD)
    k = (xm @ mxq(f64(wk), 0, "e4m3")).reshape(T, KV, HD)
    v = (xm @ mxq(f64(wv), 0, "e4m3")).reshape(T, KV, HD)
    c, s = f64(freqs_cos), f64(freqs_sin)
    return apply_rope(q, c, s), apply_rope(k, c, s), v

@@ -1,0 +1,264 @@
+from contextlib import ExitStack
+
+import concourse.mybir as mybir
+from concourse.masks import make_identity
+
+T, DIM = 2048, 1024
+NQ, NKV, HD = 1024, 256, 128
+FLOPS = 2 * T * DIM * (NQ + 2 * NKV)
+
+F32 = mybir.dt.float32
+BF16 = mybir.dt.bfloat16
+U32 = mybir.dt.uint32
+U8 = mybir.dt.uint8
+E5M2X4 = mybir.dt.float8_e5m2_x4
+E4M3X4 = mybir.dt.float8_e4m3fn_x4
+MULT = mybir.AluOpType.mult
+ADD = mybir.AluOpType.add
+
+P = 128
+PACK = 4
+K_PASS = P * PACK
+PASSES = DIM // K_PASS
+TILES = T // P
+N = 512
+PAIRS = HD // 2
+ROT = NQ + NKV
+LAG = (0, 8, 12)
+STEPS = TILES + LAG[2]
+EARLY_TILES = 4
+HEAD_VECTOR_COLS = 352
+VECTOR_ADD_COLS = 64
+PIECE = 128
+PIECES = PASSES * N // PIECE
+
+
+def tile_attention_pa_kernel(tc, x, freqs_cos, freqs_sin, wq, wk, wv, out_0, out_1, out_2):
+    nc = tc.nc
+    x_hbm = x.rearrange("(p i) k -> p i k", i=TILES)
+    cos_hbm = freqs_cos.rearrange("(p i) j -> p i j", i=TILES)
+    sin_hbm = freqs_sin.rearrange("(p i) j -> p i j", i=TILES)
+    q_hbm = out_0.rearrange("(p i) h d -> p i (h d)", i=TILES)
+    k_hbm = out_1.rearrange("(p i) h d -> p i (h d)", i=TILES)
+    v_hbm = out_2.rearrange("(p i) h d -> p i (h d)", i=TILES)
+    wq_hbm = wq.rearrange("(g p t) n -> p g t n", g=PASSES, t=PACK)
+    wk_hbm = wk.rearrange("(g p t) n -> p g t n", g=PASSES, t=PACK)
+    wv_hbm = wv.rearrange("(g p t) n -> p g t n", g=PASSES, t=PACK)
+
+    with ExitStack() as ctx:
+        keep = ctx.enter_context(tc.tile_pool(name="keep", bufs=1))
+        flow = ctx.enter_context(tc.tile_pool(name="flow", bufs=3))
+        psum = ctx.enter_context(tc.psum_pool(name="psum", bufs=2))
+        ctx.enter_context(tc.manual_schedule())
+
+        ident = keep.tile([P, P], F32, name="ident")
+        make_identity(nc, ident[:])
+
+        x_rows = {}
+        w_rows = {}
+        trig = {}
+
+        def load_x(first, count):
+            rows = keep.tile([P, count, DIM], BF16, name="x_rows%d" % first)
+            nc.sync.dma_start(out=rows[:], in_=x_hbm[:, first : first + count, :])
+            for i in range(count):
+                x_rows[first + i] = rows[:, i, :]
+
+        def load_wq(chunk, g):
+            rows = keep.tile([P, PACK, N], BF16, name="wq_rows%d_%d" % (chunk, g))
+            nc.sync.dma_start(out=rows[:], in_=wq_hbm[:, g, :, chunk * N : (chunk + 1) * N])
+            for c in range(0, N, PIECE):
+                w_rows[chunk, g, c] = rows[:, :, c:]
+
+        def load_wkv(w_hbm, col0):
+            rows = keep.tile([P, PASSES, PACK, NKV], BF16, name="wkv_rows%d" % col0)
+            nc.sync.dma_start(out=rows[:], in_=w_hbm)
+            for g in range(PASSES):
+                for c in range(0, NKV, PIECE):
+                    w_rows[2, g, col0 + c] = rows[:, g, :, c:]
+
+        def load_trig(first, count):
+            cos = keep.tile([P, count, PAIRS], BF16, name="cos%d" % first)
+            sin = keep.tile([P, 2, count, PAIRS], BF16, name="sin%d" % first)
+            nc.sync.dma_start(out=cos[:], in_=cos_hbm[:, first : first + count, :])
+            nc.sync.dma_start(out=sin[:, 1, :, :], in_=sin_hbm[:, first : first + count, :])
+            for i in range(count):
+                trig[first + i] = (cos[:, i, :], sin[:, :, i, :])
+            return sin
+
+        load_x(0, 1)
+        load_wq(0, 0)
+        load_wq(0, 1)
+        sin_early = load_trig(0, EARLY_TILES)
+        load_x(1, 1)
+        load_x(2, 1)
+        load_x(3, 1)
+        load_wq(1, 0)
+        load_x(4, 1)
+        load_x(5, 1)
+        load_wq(1, 1)
+        sin_late = load_trig(EARLY_TILES, TILES - EARLY_TILES)
+        load_x(6, 2)
+        load_wkv(wk_hbm, 0)
+        load_x(8, 2)
+        load_wkv(wv_hbm, NKV)
+        load_x(10, 2)
+        load_x(12, 2)
+        load_x(14, 2)
+
+        w_grouped = [keep.tile([P, PASSES, N, PACK], BF16, name="w_grouped%d" % c, align_bytes=64) for c in range(3)]
+        w_codes = [keep.tile([P, PASSES, N], U32, name="w_codes%d" % c, align_bytes=64) for c in range(3)]
+        w_scales = [keep.tile([P, PASSES, N], U8, name="w_scales%d" % c, align_bytes=64) for c in range(3)]
+        x_codes = [keep.tile([P, PASSES * P], U32, name="x_codes%d" % i, align_bytes=64) for i in range(TILES)]
+        x_scales = [keep.tile([P, PASSES * P], U8, name="x_scales%d" % i, align_bytes=64) for i in range(TILES)]
+
+        def group_w(copy, chunk, g, src, c0, c1):
+            copy(
+                out=w_grouped[chunk][:, g, c0:c1, :].rearrange("p (c i) t -> p c t i", i=4),
+                in_=src[:, :, 0 : c1 - c0].rearrange("p t (c i) -> p c t i", i=4),
+            )
+
+        def quantize_w(chunk, g0, g1):
+            nc.vector.quantize_mx(
+                out=w_codes[chunk][:, g0:g1, :].rearrange("p g n -> p (g n)").bitcast(E4M3X4),
+                scales=w_scales[chunk][:, g0:g1, :].rearrange("p g n -> p (g n)"),
+                in_=w_grouped[chunk][:, g0:g1, :, :].rearrange("p g n t -> p (g n t)"),
+            )
+
+        x_turned = {}
+        x_grouped = {}
+
+        def transpose_x(i):
+            words = x_rows[i].bitcast(F32)
+            turned = psum.tile([P, PASSES, 2, P], F32, name="turned")
+            for g in range(PASSES):
+                for u in range(2):
+                    nc.tensor.transpose(turned[:, g, u, :], words[:, 2 * P * g + u : 2 * P * (g + 1) : 2], ident[:])
+            x_turned[i] = turned
+
+        def group_x(i):
+            grouped = flow.tile([P, PASSES * P * PACK], BF16, name="grouped", align_bytes=64)
+            nc.scalar.copy(
+                out=grouped[:].bitcast(F32).rearrange("p (g r u) -> p g r u", g=PASSES, u=2),
+                in_=x_turned[i][:].rearrange("p g u r -> p g r u"),
+            )
+            x_grouped[i] = grouped
+
+        def quantize_x(i):
+            nc.vector.quantize_mx(out=x_codes[i][:].bitcast(E5M2X4), scales=x_scales[i][:], in_=x_grouped[i][:])
+
+        def negate_sin(sin):
+            nc.vector.tensor_scalar_mul(sin[:, 0, :, :], sin[:, 1, :, :], -1.0)
+
+        sums = {}
+
+        def project(chunk, i):
+            acc = psum.tile([P, N], F32, name="acc%d" % chunk)
+            for g in range(PASSES):
+                nc.tensor.matmul_mx(
+                    out=acc[:],
+                    lhsT=x_codes[i][:, g * P : (g + 1) * P].bitcast(E5M2X4),
+                    lhsT_scale=x_scales[i][:, g * P : (g + 1) * P],
+                    rhs=w_codes[chunk][:, g, :].bitcast(E4M3X4),
+                    rhs_scale=w_scales[chunk][:, g, :],
+                    start=(g == 0),
+                    stop=(g == PASSES - 1),
+                )
+            sums[chunk, i] = acc
+
+        def store_v(i):
+            v_sb = flow.tile([P, NKV], F32, name="v_sb", bufs=4)
+            nc.scalar.copy(out=v_sb[:], in_=sums[2, i][:, NKV:])
+            return v_sb
+
+        def products(chunk, i, by_cos, by_sin):
+            width = by_cos.shape[1]
+            shape = [P, width // HD, PAIRS, 2]
+            cos, sin = trig[i]
+            u = sums[chunk, i][:, :width].rearrange("p (h j e) -> p h j e", j=PAIRS, e=2)
+            nc.vector.tensor_tensor(
+                out=by_cos.rearrange("p (h j e) -> p h j e", j=PAIRS, e=2),
+                in0=u,
+                in1=cos.unsqueeze(1).unsqueeze(3).broadcast_to(shape),
+                op=MULT,
+            )
+            nc.vector.tensor_tensor(
+                out=by_sin.rearrange("p (h j e) -> p h j e", j=PAIRS, e=2),
+                in0=u[:, :, :, ::-1],
+                in1=sin.rearrange("p e j -> p j e").unsqueeze(1).broadcast_to(shape),
+                op=MULT,
+            )
+
+        def units(step):
+            return [(c, step - LAG[c]) for c in range(3) if 0 <= step - LAG[c] < TILES]
+
+        split = HEAD_VECTOR_COLS
+        transpose_x(0)
+        group_x(0)
+        group_w(nc.vector.tensor_copy, 0, 0, w_rows[0, 0, 0], 0, split)
+        group_w(nc.scalar.copy, 0, 0, w_rows[0, 0, 0][:, :, split:], split, N)
+        quantize_x(0)
+        group_w(nc.vector.tensor_copy, 0, 1, w_rows[0, 1, 0], 0, split)
+        group_w(nc.scalar.copy, 0, 1, w_rows[0, 1, 0][:, :, split:], split, N)
+        transpose_x(1)
+        group_x(1)
+        quantize_w(0, 0, 1)
+        negate_sin(sin_early)
+        quantize_w(0, 1, 2)
+        project(0, 0)
+        quantize_x(1)
+        transpose_x(2)
+        group_x(2)
+
+        pieces = {}
+        first = 0
+        for chunk in (1, 2):
+            span = LAG[chunk] - 2 - first
+            for n in range(PIECES):
+                pieces.setdefault(first + n * span // PIECES, []).append((chunk, n))
+            first += span
+
+        v_ready = {}
+        for step in range(STEPS):
+            for chunk, i in units(step + 1):
+                project(chunk, i)
+            if step + 3 < TILES:
+                transpose_x(step + 3)
+            for chunk, n in pieces.get(step, []):
+                g, c0 = divmod(n * PIECE, N)
+                if chunk == 2:
+                    g, c0 = (n // 2) % 2, (n // 4) * NKV + (n % 2) * PIECE
+                group_w(nc.scalar.copy, chunk, g, w_rows[chunk, g, c0], c0, c0 + PIECE)
+            for chunk, i in units(step + 1):
+                if chunk == 2:
+                    v_ready[i] = store_v(i)
+            if step + 3 < TILES:
+                group_x(step + 3)
+
+            rot = flow.tile([P, ROT], F32, name="rot", bufs=10)
+            by_sin = flow.tile([P, ROT], F32, name="by_sin")
+            cols = {}
+            for chunk, i in units(step):
+                cols[chunk] = slice(chunk * N, min((chunk + 1) * N, ROT))
+                products(chunk, i, rot[:, cols[chunk]], by_sin[:, cols[chunk]])
+            lo = min(c.start for c in cols.values())
+            hi = max(c.stop for c in cols.values())
+            cut = lo if step == STEPS - 1 else hi - VECTOR_ADD_COLS
+
+            if step + 2 < TILES:
+                quantize_x(step + 2)
+            for chunk in (1, 2):
+                if step == LAG[chunk] - 2:
+                    quantize_w(chunk, 0, PASSES)
+            if step == EARLY_TILES - 2:
+                negate_sin(sin_late)
+            nc.vector.tensor_tensor(out=rot[:, cut:hi], in0=rot[:, cut:hi], in1=by_sin[:, cut:hi], op=ADD)
+            if cut > lo:
+                nc.gpsimd.tensor_tensor(out=rot[:, lo:cut], in0=rot[:, lo:cut], in1=by_sin[:, lo:cut], op=ADD)
+
+            for chunk, i in units(step):
+                if chunk < 2:
+                    nc.sync.dma_start(out=q_hbm[:, i, cols[chunk]], in_=rot[:, cols[chunk]])
+                else:
+                    nc.sync.dma_start(out=v_hbm[:, i, :], in_=v_ready[i][:])
+                    nc.sync.dma_start(out=k_hbm[:, i, :], in_=rot[:, cols[chunk]])

@@ -24,11 +24,11 @@ TILES = T // P
 N = 512
 PAIRS = HD // 2
 ROT = NQ + NKV
-LAG = (0, 8, 12)
-STEPS = TILES + LAG[2]
-EARLY_TILES = 4
+ACC_BANKS = 6
+ROUND_COLS = 3 * N
+EARLY_TILES = 6
 HEAD_VECTOR_COLS = 352
-VECTOR_ADD_COLS = 64
+VECTOR_ADD_COLS = 160
 PIECE = 128
 PIECES = PASSES * N // PIECE
 
@@ -86,31 +86,28 @@ def tile_attention_pa_kernel(tc, x, freqs_cos, freqs_sin, wq, wk, wv, out_0, out
                 trig[first + i] = (cos[:, i, :], sin[:, :, i, :])
             return sin
 
-        load_x(0, 1)
         load_wq(0, 0)
+        load_x(0, 1)
         load_wq(0, 1)
         sin_early = load_trig(0, EARLY_TILES)
-        load_x(1, 1)
-        load_x(2, 1)
-        load_x(3, 1)
+        for i in range(1, 6):
+            load_x(i, 1)
         load_wq(1, 0)
-        load_x(4, 1)
-        load_x(5, 1)
+        load_x(6, 2)
         load_wq(1, 1)
         sin_late = load_trig(EARLY_TILES, TILES - EARLY_TILES)
-        load_x(6, 2)
-        load_wkv(wk_hbm, 0)
         load_x(8, 2)
-        load_wkv(wv_hbm, NKV)
+        load_wkv(wk_hbm, 0)
         load_x(10, 2)
+        load_wkv(wv_hbm, NKV)
         load_x(12, 2)
         load_x(14, 2)
 
         w_grouped = [keep.tile([P, PASSES, N, PACK], BF16, name="w_grouped%d" % c, align_bytes=64) for c in range(3)]
         w_codes = [keep.tile([P, PASSES, N], U32, name="w_codes%d" % c, align_bytes=64) for c in range(3)]
         w_scales = [keep.tile([P, PASSES, N], U8, name="w_scales%d" % c, align_bytes=64) for c in range(3)]
-        x_codes = [keep.tile([P, PASSES * P], U32, name="x_codes%d" % i, align_bytes=64) for i in range(TILES)]
-        x_scales = [keep.tile([P, PASSES * P], U8, name="x_scales%d" % i, align_bytes=64) for i in range(TILES)]
+        x_codes = [keep.tile([P, 2, PASSES * P], U32, name="x_codes%d" % m, align_bytes=64) for m in range(TILES // 2)]
+        x_scales = [keep.tile([P, 2, PASSES * P], U8, name="x_scales%d" % m, align_bytes=64) for m in range(TILES // 2)]
 
         def group_w(copy, chunk, g, src, c0, c1):
             copy(
@@ -125,6 +122,7 @@ def tile_attention_pa_kernel(tc, x, freqs_cos, freqs_sin, wq, wk, wv, out_0, out
                 in_=w_grouped[chunk][:, g0:g1, :, :].rearrange("p g n t -> p (g n t)"),
             )
 
+        quantized = set()
         x_turned = {}
         x_grouped = {}
 
@@ -137,15 +135,22 @@ def tile_attention_pa_kernel(tc, x, freqs_cos, freqs_sin, wq, wk, wv, out_0, out
             x_turned[i] = turned
 
         def group_x(i):
-            grouped = flow.tile([P, PASSES * P * PACK], BF16, name="grouped", align_bytes=64)
+            if i % 2 == 0:
+                x_grouped[i // 2] = flow.tile([P, 2, PASSES * P * PACK], BF16, name="grouped", align_bytes=64)
             nc.scalar.copy(
-                out=grouped[:].bitcast(F32).rearrange("p (g r u) -> p g r u", g=PASSES, u=2),
+                out=x_grouped[i // 2][:, i % 2, :].bitcast(F32).rearrange("p (g r u) -> p g r u", g=PASSES, u=2),
                 in_=x_turned[i][:].rearrange("p g u r -> p g r u"),
             )
-            x_grouped[i] = grouped
 
-        def quantize_x(i):
-            nc.vector.quantize_mx(out=x_codes[i][:].bitcast(E5M2X4), scales=x_scales[i][:], in_=x_grouped[i][:])
+        def quantize_x(first, count):
+            m, held = first // 2, slice(first % 2, first % 2 + count)
+            nc.vector.quantize_mx(
+                out=x_codes[m][:, held, :].rearrange("p i n -> p (i n)").bitcast(E5M2X4),
+                scales=x_scales[m][:, held, :].rearrange("p i n -> p (i n)"),
+                in_=x_grouped[m][:, held, :].rearrange("p i n -> p (i n)"),
+            )
+            for i in range(first, first + count):
+                quantized.add(i)
 
         def negate_sin(sin):
             nc.vector.tensor_scalar_mul(sin[:, 0, :, :], sin[:, 1, :, :], -1.0)
@@ -153,12 +158,12 @@ def tile_attention_pa_kernel(tc, x, freqs_cos, freqs_sin, wq, wk, wv, out_0, out
         sums = {}
 
         def project(chunk, i):
-            acc = psum.tile([P, N], F32, name="acc%d" % chunk)
+            acc = psum.tile([P, N], F32, name="acc", bufs=ACC_BANKS)
             for g in range(PASSES):
                 nc.tensor.matmul_mx(
                     out=acc[:],
-                    lhsT=x_codes[i][:, g * P : (g + 1) * P].bitcast(E5M2X4),
-                    lhsT_scale=x_scales[i][:, g * P : (g + 1) * P],
+                    lhsT=x_codes[i // 2][:, i % 2, g * P : (g + 1) * P].bitcast(E5M2X4),
+                    lhsT_scale=x_scales[i // 2][:, i % 2, g * P : (g + 1) * P],
                     rhs=w_codes[chunk][:, g, :].bitcast(E4M3X4),
                     rhs_scale=w_scales[chunk][:, g, :],
                     start=(g == 0),
@@ -167,7 +172,7 @@ def tile_attention_pa_kernel(tc, x, freqs_cos, freqs_sin, wq, wk, wv, out_0, out
             sums[chunk, i] = acc
 
         def store_v(i):
-            v_sb = flow.tile([P, NKV], F32, name="v_sb", bufs=4)
+            v_sb = flow.tile([P, NKV], F32, name="v_sb", bufs=8)
             nc.scalar.copy(out=v_sb[:], in_=sums[2, i][:, NKV:])
             return v_sb
 
@@ -189,76 +194,97 @@ def tile_attention_pa_kernel(tc, x, freqs_cos, freqs_sin, wq, wk, wv, out_0, out
                 op=MULT,
             )
 
-        def units(step):
-            return [(c, step - LAG[c]) for c in range(3) if 0 <= step - LAG[c] < TILES]
+        rounds = [[(0, i)] for i in range(3)] + [[(0, i), (0, i + 1)] for i in range(3, 9, 2)]
+        for m in range(7):
+            rounds.append([(0, 9 + m), (1, m)] + ([(2, 2 * m - 6), (2, 2 * m - 5)] if m >= 3 else []))
+        rounds.append([(1, 7), (1, 8), (2, 8)])
+        rounds.extend([[(1, i), (2, i), (1, i + 1), (2, i + 1)] for i in (9, 11, 13)])
+        rounds.append([(1, 15), (2, 15)])
+        order = [unit for units in rounds for unit in units]
+        width = {0: N, 1: N, 2: NKV}
+        round_cols = [sum(width[chunk] for chunk, i in units) for units in rounds] + [0]
+        w_rounds = {1: range(2, 6), 2: range(6, 9)}
+        x_due = [[2], [3]] + [[i, i + 1] for i in range(4, TILES, 2)] + [[]] * len(rounds)
 
         split = HEAD_VECTOR_COLS
-        transpose_x(0)
-        group_x(0)
         group_w(nc.vector.tensor_copy, 0, 0, w_rows[0, 0, 0], 0, split)
         group_w(nc.scalar.copy, 0, 0, w_rows[0, 0, 0][:, :, split:], split, N)
-        quantize_x(0)
+        transpose_x(0)
+        group_x(0)
+        quantize_w(0, 0, 1)
         group_w(nc.vector.tensor_copy, 0, 1, w_rows[0, 1, 0], 0, split)
         group_w(nc.scalar.copy, 0, 1, w_rows[0, 1, 0][:, :, split:], split, N)
+        quantize_x(0, 1)
+        quantize_w(0, 1, 2)
+        ready_chunks = {0}
+        negate_sin(sin_early)
         transpose_x(1)
         group_x(1)
-        quantize_w(0, 0, 1)
-        negate_sin(sin_early)
-        quantize_w(0, 1, 2)
+        quantize_x(1, 1)
         project(0, 0)
-        quantize_x(1)
         transpose_x(2)
         group_x(2)
 
         pieces = {}
-        first = 0
-        for chunk in (1, 2):
-            span = LAG[chunk] - 2 - first
+        for chunk, span in w_rounds.items():
             for n in range(PIECES):
-                pieces.setdefault(first + n * span // PIECES, []).append((chunk, n))
-            first += span
+                pieces.setdefault(span[n * len(span) // PIECES], []).append((chunk, n))
 
         v_ready = {}
-        for step in range(STEPS):
-            for chunk, i in units(step + 1):
+        projected = 1
+        consumed = 0
+        for r, units in enumerate(rounds):
+            fresh = []
+            while projected < min(len(order), consumed + ACC_BANKS):
+                chunk, i = order[projected]
+                if chunk not in ready_chunks or i not in quantized:
+                    break
                 project(chunk, i)
-            if step + 3 < TILES:
-                transpose_x(step + 3)
-            for chunk, n in pieces.get(step, []):
+                fresh.append((chunk, i))
+                projected += 1
+            ahead = x_due[r + 1]
+            for i in ahead:
+                transpose_x(i)
+            for chunk, n in pieces.get(r, []):
                 g, c0 = divmod(n * PIECE, N)
                 if chunk == 2:
                     g, c0 = (n // 2) % 2, (n // 4) * NKV + (n % 2) * PIECE
                 group_w(nc.scalar.copy, chunk, g, w_rows[chunk, g, c0], c0, c0 + PIECE)
-            for chunk, i in units(step + 1):
+            for chunk, i in fresh:
                 if chunk == 2:
                     v_ready[i] = store_v(i)
-            if step + 3 < TILES:
-                group_x(step + 3)
+            for i in ahead:
+                group_x(i)
 
-            rot = flow.tile([P, ROT], F32, name="rot", bufs=10)
-            by_sin = flow.tile([P, ROT], F32, name="by_sin")
-            cols = {}
-            for chunk, i in units(step):
-                cols[chunk] = slice(chunk * N, min((chunk + 1) * N, ROT))
-                products(chunk, i, rot[:, cols[chunk]], by_sin[:, cols[chunk]])
-            lo = min(c.start for c in cols.values())
-            hi = max(c.stop for c in cols.values())
-            cut = lo if step == STEPS - 1 else hi - VECTOR_ADD_COLS
+            rot = flow.tile([P, ROUND_COLS], F32, name="rot", bufs=7)
+            by_sin = flow.tile([P, ROUND_COLS], F32, name="by_sin")
+            cols = []
+            for chunk, i in units:
+                start = cols[-1].stop if cols else 0
+                cols.append(slice(start, start + width[chunk]))
+                products(chunk, i, rot[:, cols[-1]], by_sin[:, cols[-1]])
+            consumed += len(units)
 
-            if step + 2 < TILES:
-                quantize_x(step + 2)
-            for chunk in (1, 2):
-                if step == LAG[chunk] - 2:
+            if x_due[r]:
+                quantize_x(x_due[r][0], len(x_due[r]))
+            for chunk, span in w_rounds.items():
+                if r == span[-1]:
                     quantize_w(chunk, 0, PASSES)
-            if step == EARLY_TILES - 2:
+                    ready_chunks.add(chunk)
+            if r == 3:
                 negate_sin(sin_late)
-            nc.vector.tensor_tensor(out=rot[:, cut:hi], in0=rot[:, cut:hi], in1=by_sin[:, cut:hi], op=ADD)
-            if cut > lo:
-                nc.gpsimd.tensor_tensor(out=rot[:, lo:cut], in0=rot[:, lo:cut], in1=by_sin[:, lo:cut], op=ADD)
+            total = round_cols[r]
+            cut = max(0, min(total, VECTOR_ADD_COLS + total - round_cols[r + 1]))
+            for c in cols:
+                if c.start < cut:
+                    mine = slice(c.start, min(c.stop, cut))
+                    nc.vector.tensor_tensor(out=rot[:, mine], in0=rot[:, mine], in1=by_sin[:, mine], op=ADD)
+            if cut < total:
+                nc.gpsimd.tensor_tensor(out=rot[:, cut:total], in0=rot[:, cut:total], in1=by_sin[:, cut:total], op=ADD)
 
-            for chunk, i in units(step):
+            for (chunk, i), c in zip(units, cols):
                 if chunk < 2:
-                    nc.sync.dma_start(out=q_hbm[:, i, cols[chunk]], in_=rot[:, cols[chunk]])
+                    nc.sync.dma_start(out=q_hbm[:, i, chunk * N : (chunk + 1) * N], in_=rot[:, c])
                 else:
                     nc.sync.dma_start(out=v_hbm[:, i, :], in_=v_ready[i][:])
-                    nc.sync.dma_start(out=k_hbm[:, i, :], in_=rot[:, cols[chunk]])
+                    nc.sync.dma_start(out=k_hbm[:, i, :], in_=rot[:, c])

@@ -25,10 +25,11 @@ N = 512
 PAIRS = HD // 2
 ROT = NQ + NKV
 ACC_BANKS = 6
-ROUND_COLS = 3 * N
+ROUND_COLS = 2 * N + NKV
+TAIL_TILES = 3
 EARLY_TILES = 6
 HEAD_VECTOR_COLS = 352
-VECTOR_ADD_COLS = 160
+VECTOR_ADD_COLS = 384
 PIECE = 128
 PIECES = PASSES * N // PIECE
 
@@ -83,7 +84,7 @@ def tile_attention_pa_kernel(tc, x, freqs_cos, freqs_sin, wq, wk, wv, out_0, out
             nc.sync.dma_start(out=cos[:], in_=cos_hbm[:, first : first + count, :])
             nc.sync.dma_start(out=sin[:, 1, :, :], in_=sin_hbm[:, first : first + count, :])
             for i in range(count):
-                trig[first + i] = (cos[:, i, :], sin[:, :, i, :])
+                trig[first + i] = (cos[:, i:, :], sin[:, :, i:, :])
             return sin
 
         load_wq(0, 0)
@@ -174,36 +175,51 @@ def tile_attention_pa_kernel(tc, x, freqs_cos, freqs_sin, wq, wk, wv, out_0, out
         def store_v(i):
             v_sb = flow.tile([P, NKV], F32, name="v_sb", bufs=8)
             nc.scalar.copy(out=v_sb[:], in_=sums[2, i][:, NKV:])
-            return v_sb
+            nc.sync.dma_start(out=v_hbm[:, i, :], in_=v_sb[:])
 
-        def products(chunk, i, by_cos, by_sin):
-            width = by_cos.shape[1]
-            shape = [P, width // HD, PAIRS, 2]
-            cos, sin = trig[i]
-            u = sums[chunk, i][:, :width].rearrange("p (h j e) -> p h j e", j=PAIRS, e=2)
+        cos_pairs = keep.tile([P, TILES, HD], BF16, name="cos_pairs")
+        sin_pairs = keep.tile([P, TILES, HD], BF16, name="sin_pairs")
+
+        def pair_trig(first, count):
+            cos, sin = trig[first]
+            held = slice(first, first + count)
+            nc.scalar.copy(
+                out=cos_pairs[:, held, :].rearrange("p i (j e) -> p i j e", e=2),
+                in_=cos[:, :count, :].unsqueeze(3).broadcast_to([P, count, PAIRS, 2]),
+            )
+            nc.scalar.copy(
+                out=sin_pairs[:, held, :].rearrange("p i (j e) -> p i j e", e=2),
+                in_=sin[:, :, :count, :].rearrange("p e i j -> p i j e"),
+            )
+
+        def times_cos(chunk, i, out):
+            heads = out.shape[1] // HD
             nc.vector.tensor_tensor(
-                out=by_cos.rearrange("p (h j e) -> p h j e", j=PAIRS, e=2),
-                in0=u,
-                in1=cos.unsqueeze(1).unsqueeze(3).broadcast_to(shape),
+                out=out.rearrange("p (h d) -> p h d", d=HD),
+                in0=sums[chunk, i][:, : heads * HD].rearrange("p (h d) -> p h d", d=HD),
+                in1=cos_pairs[:, i, :].unsqueeze(1).broadcast_to([P, heads, HD]),
                 op=MULT,
             )
+
+        def times_sin(chunk, i, out, h0, h1):
+            cols = slice(h0 * HD, h1 * HD)
             nc.vector.tensor_tensor(
-                out=by_sin.rearrange("p (h j e) -> p h j e", j=PAIRS, e=2),
-                in0=u[:, :, :, ::-1],
-                in1=sin.rearrange("p e j -> p j e").unsqueeze(1).broadcast_to(shape),
+                out=out[:, cols].rearrange("p (h j e) -> p h j e", j=PAIRS, e=2),
+                in0=sums[chunk, i][:, cols].rearrange("p (h j e) -> p h j e", j=PAIRS, e=2)[:, :, :, ::-1],
+                in1=sin_pairs[:, i, :].rearrange("p (j e) -> p j e", e=2).unsqueeze(1).broadcast_to([P, h1 - h0, PAIRS, 2]),
                 op=MULT,
             )
 
         rounds = [[(0, i)] for i in range(3)] + [[(0, i), (0, i + 1)] for i in range(3, 9, 2)]
-        for m in range(7):
-            rounds.append([(0, 9 + m), (1, m)] + ([(2, 2 * m - 6), (2, 2 * m - 5)] if m >= 3 else []))
-        rounds.append([(1, 7), (1, 8), (2, 8)])
-        rounds.extend([[(1, i), (2, i), (1, i + 1), (2, i + 1)] for i in (9, 11, 13)])
-        rounds.append([(1, 15), (2, 15)])
+        rounds += [[(0, 9 + m), (1, m)] for m in range(2)]
+        rounds += [[(0, 9 + m), (1, m), (2, m - 2)] for m in range(2, 7)]
+        rounds += [[(1, 7 + m), (2, 5 + 2 * m), (2, 6 + 2 * m)] for m in range(2)]
+        rounds += [[(1, i), (2, i)] for i in range(9, TILES - TAIL_TILES)]
+        rounds += [[(c, i) for i in range(TILES - TAIL_TILES, TILES) for c in (1, 2)]]
         order = [unit for units in rounds for unit in units]
         width = {0: N, 1: N, 2: NKV}
         round_cols = [sum(width[chunk] for chunk, i in units) for units in rounds] + [0]
-        w_rounds = {1: range(2, 6), 2: range(6, 9)}
+        w_due = {5: 1, 7: 2}
         x_due = [[2], [3]] + [[i, i + 1] for i in range(4, TILES, 2)] + [[]] * len(rounds)
 
         split = HEAD_VECTOR_COLS
@@ -214,10 +230,11 @@ def tile_attention_pa_kernel(tc, x, freqs_cos, freqs_sin, wq, wk, wv, out_0, out
         quantize_w(0, 0, 1)
         group_w(nc.vector.tensor_copy, 0, 1, w_rows[0, 1, 0], 0, split)
         group_w(nc.scalar.copy, 0, 1, w_rows[0, 1, 0][:, :, split:], split, N)
+        negate_sin(sin_early)
         quantize_x(0, 1)
         quantize_w(0, 1, 2)
         ready_chunks = {0}
-        negate_sin(sin_early)
+        pair_trig(0, 2)
         transpose_x(1)
         group_x(1)
         quantize_x(1, 1)
@@ -225,12 +242,12 @@ def tile_attention_pa_kernel(tc, x, freqs_cos, freqs_sin, wq, wk, wv, out_0, out
         transpose_x(2)
         group_x(2)
 
+        piece_rounds = range(3, 8)
         pieces = {}
-        for chunk, span in w_rounds.items():
-            for n in range(PIECES):
-                pieces.setdefault(span[n * len(span) // PIECES], []).append((chunk, n))
+        for n in range(2 * PIECES):
+            r = piece_rounds[min(n // 3, len(piece_rounds) - 1)]
+            pieces.setdefault(r, []).append((1 + n // PIECES, n % PIECES))
 
-        v_ready = {}
         projected = 1
         consumed = 0
         for r, units in enumerate(rounds):
@@ -245,6 +262,8 @@ def tile_attention_pa_kernel(tc, x, freqs_cos, freqs_sin, wq, wk, wv, out_0, out
             ahead = x_due[r + 1]
             for i in ahead:
                 transpose_x(i)
+            if x_due[r]:
+                pair_trig(x_due[r][0], len(x_due[r]))
             for chunk, n in pieces.get(r, []):
                 g, c0 = divmod(n * PIECE, N)
                 if chunk == 2:
@@ -252,33 +271,43 @@ def tile_attention_pa_kernel(tc, x, freqs_cos, freqs_sin, wq, wk, wv, out_0, out
                 group_w(nc.scalar.copy, chunk, g, w_rows[chunk, g, c0], c0, c0 + PIECE)
             for chunk, i in fresh:
                 if chunk == 2:
-                    v_ready[i] = store_v(i)
+                    store_v(i)
             for i in ahead:
                 group_x(i)
 
-            rot = flow.tile([P, ROUND_COLS], F32, name="rot", bufs=7)
-            by_sin = flow.tile([P, ROUND_COLS], F32, name="by_sin")
+            total = round_cols[r]
+            last = r == len(rounds) - 1
+            if last:
+                rot = keep.tile([P, total], F32, name="rot_tail")
+                by_sin = keep.tile([P, total], F32, name="by_sin_tail")
+                cut = total
+            else:
+                rot = flow.tile([P, ROUND_COLS], F32, name="rot", bufs=7)
+                by_sin = flow.tile([P, ROUND_COLS], F32, name="by_sin", bufs=4)
+                cut = max(0, VECTOR_ADD_COLS + total - round_cols[r + 1]) if x_due[r + 1] else 0
             cols = []
             for chunk, i in units:
                 start = cols[-1].stop if cols else 0
                 cols.append(slice(start, start + width[chunk]))
-                products(chunk, i, rot[:, cols[-1]], by_sin[:, cols[-1]])
+                heads = width[chunk] // HD
+                held_back = 1 if x_due[r] and (chunk, i) == units[-1] else 0
+                times_cos(chunk, i, rot[:, cols[-1]])
+                times_sin(chunk, i, by_sin[:, cols[-1]], 0, heads - held_back)
             consumed += len(units)
 
             if x_due[r]:
                 quantize_x(x_due[r][0], len(x_due[r]))
-            for chunk, span in w_rounds.items():
-                if r == span[-1]:
-                    quantize_w(chunk, 0, PASSES)
-                    ready_chunks.add(chunk)
-            if r == 3:
+            if r in w_due:
+                quantize_w(w_due[r], 0, PASSES)
+                ready_chunks.add(w_due[r])
+            if r == 2:
                 negate_sin(sin_late)
-            total = round_cols[r]
-            cut = max(0, min(total, VECTOR_ADD_COLS + total - round_cols[r + 1]))
             for c in cols:
                 if c.start < cut:
                     mine = slice(c.start, min(c.stop, cut))
                     nc.vector.tensor_tensor(out=rot[:, mine], in0=rot[:, mine], in1=by_sin[:, mine], op=ADD)
+            if x_due[r]:
+                times_sin(chunk, i, by_sin[:, cols[-1]], heads - 1, heads)
             if cut < total:
                 nc.gpsimd.tensor_tensor(out=rot[:, cut:total], in0=rot[:, cut:total], in1=by_sin[:, cut:total], op=ADD)
 
@@ -286,5 +315,4 @@ def tile_attention_pa_kernel(tc, x, freqs_cos, freqs_sin, wq, wk, wv, out_0, out
                 if chunk < 2:
                     nc.sync.dma_start(out=q_hbm[:, i, chunk * N : (chunk + 1) * N], in_=rot[:, c])
                 else:
-                    nc.sync.dma_start(out=v_hbm[:, i, :], in_=v_ready[i][:])
                     nc.sync.dma_start(out=k_hbm[:, i, :], in_=rot[:, c])

@@ -26,7 +26,7 @@ PAIRS = HD // 2
 ROT = NQ + NKV
 ACC_BANKS = 6
 ROUND_COLS = 2 * N + NKV
-TAIL_TILES = 3
+FIRST_TENSOR_ADD_ROUND = 5
 EARLY_TILES = 6
 HEAD_VECTOR_COLS = 352
 VECTOR_ADD_COLS = 384
@@ -90,25 +90,26 @@ def tile_attention_pa_kernel(tc, x, freqs_cos, freqs_sin, wq, wk, wv, out_0, out
         load_wq(0, 0)
         load_x(0, 1)
         load_wq(0, 1)
-        sin_early = load_trig(0, EARLY_TILES)
-        for i in range(1, 6):
-            load_x(i, 1)
+        load_x(1, 1)
+        load_x(2, 1)
+        sin_all = load_trig(0, TILES)
+        load_x(3, 1)
+        load_x(4, 1)
+        load_x(5, 2)
         load_wq(1, 0)
-        load_x(6, 2)
+        load_x(7, 2)
         load_wq(1, 1)
-        sin_late = load_trig(EARLY_TILES, TILES - EARLY_TILES)
-        load_x(8, 2)
+        load_x(9, 2)
         load_wkv(wk_hbm, 0)
-        load_x(10, 2)
+        load_x(11, 2)
         load_wkv(wv_hbm, NKV)
-        load_x(12, 2)
-        load_x(14, 2)
+        load_x(13, 3)
 
         w_grouped = [keep.tile([P, PASSES, N, PACK], BF16, name="w_grouped%d" % c, align_bytes=64) for c in range(3)]
         w_codes = [keep.tile([P, PASSES, N], U32, name="w_codes%d" % c, align_bytes=64) for c in range(3)]
         w_scales = [keep.tile([P, PASSES, N], U8, name="w_scales%d" % c, align_bytes=64) for c in range(3)]
-        x_codes = [keep.tile([P, 2, PASSES * P], U32, name="x_codes%d" % m, align_bytes=64) for m in range(TILES // 2)]
-        x_scales = [keep.tile([P, 2, PASSES * P], U8, name="x_scales%d" % m, align_bytes=64) for m in range(TILES // 2)]
+        x_groups = [[0], [1], [2]] + [[i, i + 1] for i in range(3, TILES - 1, 2)] + [[TILES - 1]]
+        x_group_of = {i: group for group in x_groups for i in group}
 
         def group_w(copy, chunk, g, src, c0, c1):
             copy(
@@ -123,7 +124,7 @@ def tile_attention_pa_kernel(tc, x, freqs_cos, freqs_sin, wq, wk, wv, out_0, out
                 in_=w_grouped[chunk][:, g0:g1, :, :].rearrange("p g n t -> p (g n t)"),
             )
 
-        quantized = set()
+        x_mx = {}
         x_turned = {}
         x_grouped = {}
 
@@ -136,22 +137,24 @@ def tile_attention_pa_kernel(tc, x, freqs_cos, freqs_sin, wq, wk, wv, out_0, out
             x_turned[i] = turned
 
         def group_x(i):
-            if i % 2 == 0:
-                x_grouped[i // 2] = flow.tile([P, 2, PASSES * P * PACK], BF16, name="grouped", align_bytes=64)
+            group = x_group_of[i]
+            if i == group[0]:
+                x_grouped[i] = flow.tile([P, len(group), PASSES * P * PACK], BF16, name="grouped", align_bytes=64)
             nc.scalar.copy(
-                out=x_grouped[i // 2][:, i % 2, :].bitcast(F32).rearrange("p (g r u) -> p g r u", g=PASSES, u=2),
+                out=x_grouped[group[0]][:, i - group[0], :].bitcast(F32).rearrange("p (g r u) -> p g r u", g=PASSES, u=2),
                 in_=x_turned[i][:].rearrange("p g u r -> p g r u"),
             )
 
-        def quantize_x(first, count):
-            m, held = first // 2, slice(first % 2, first % 2 + count)
+        def quantize_x(group):
+            codes = keep.tile([P, len(group), PASSES * P], U32, name="x_codes%d" % group[0], align_bytes=64)
+            scales = keep.tile([P, len(group), PASSES * P], U8, name="x_scales%d" % group[0], align_bytes=64)
             nc.vector.quantize_mx(
-                out=x_codes[m][:, held, :].rearrange("p i n -> p (i n)").bitcast(E5M2X4),
-                scales=x_scales[m][:, held, :].rearrange("p i n -> p (i n)"),
-                in_=x_grouped[m][:, held, :].rearrange("p i n -> p (i n)"),
+                out=codes[:].rearrange("p i n -> p (i n)").bitcast(E5M2X4),
+                scales=scales[:].rearrange("p i n -> p (i n)"),
+                in_=x_grouped[group[0]][:].rearrange("p i n -> p (i n)"),
             )
-            for i in range(first, first + count):
-                quantized.add(i)
+            for i in group:
+                x_mx[i] = (codes[:, i - group[0], :], scales[:, i - group[0], :])
 
         def negate_sin(sin):
             nc.vector.tensor_scalar_mul(sin[:, 0, :, :], sin[:, 1, :, :], -1.0)
@@ -163,8 +166,8 @@ def tile_attention_pa_kernel(tc, x, freqs_cos, freqs_sin, wq, wk, wv, out_0, out
             for g in range(PASSES):
                 nc.tensor.matmul_mx(
                     out=acc[:],
-                    lhsT=x_codes[i // 2][:, i % 2, g * P : (g + 1) * P].bitcast(E5M2X4),
-                    lhsT_scale=x_scales[i // 2][:, i % 2, g * P : (g + 1) * P],
+                    lhsT=x_mx[i][0][:, g * P : (g + 1) * P].bitcast(E5M2X4),
+                    lhsT_scale=x_mx[i][1][:, g * P : (g + 1) * P],
                     rhs=w_codes[chunk][:, g, :].bitcast(E4M3X4),
                     rhs_scale=w_scales[chunk][:, g, :],
                     start=(g == 0),
@@ -173,31 +176,16 @@ def tile_attention_pa_kernel(tc, x, freqs_cos, freqs_sin, wq, wk, wv, out_0, out
             sums[chunk, i] = acc
 
         def store_v(i):
-            v_sb = flow.tile([P, NKV], F32, name="v_sb", bufs=8)
+            v_sb = flow.tile([P, NKV], F32, name="v_sb", bufs=4)
             nc.scalar.copy(out=v_sb[:], in_=sums[2, i][:, NKV:])
             nc.sync.dma_start(out=v_hbm[:, i, :], in_=v_sb[:])
-
-        cos_pairs = keep.tile([P, TILES, HD], BF16, name="cos_pairs")
-        sin_pairs = keep.tile([P, TILES, HD], BF16, name="sin_pairs")
-
-        def pair_trig(first, count):
-            cos, sin = trig[first]
-            held = slice(first, first + count)
-            nc.scalar.copy(
-                out=cos_pairs[:, held, :].rearrange("p i (j e) -> p i j e", e=2),
-                in_=cos[:, :count, :].unsqueeze(3).broadcast_to([P, count, PAIRS, 2]),
-            )
-            nc.scalar.copy(
-                out=sin_pairs[:, held, :].rearrange("p i (j e) -> p i j e", e=2),
-                in_=sin[:, :, :count, :].rearrange("p e i j -> p i j e"),
-            )
 
         def times_cos(chunk, i, out):
             heads = out.shape[1] // HD
             nc.vector.tensor_tensor(
-                out=out.rearrange("p (h d) -> p h d", d=HD),
-                in0=sums[chunk, i][:, : heads * HD].rearrange("p (h d) -> p h d", d=HD),
-                in1=cos_pairs[:, i, :].unsqueeze(1).broadcast_to([P, heads, HD]),
+                out=out.rearrange("p (h j e) -> p h j e", j=PAIRS, e=2),
+                in0=sums[chunk, i][:, : heads * HD].rearrange("p (h j e) -> p h j e", j=PAIRS, e=2),
+                in1=trig[i][0][:, 0, :].unsqueeze(1).unsqueeze(3).broadcast_to([P, heads, PAIRS, 2]),
                 op=MULT,
             )
 
@@ -206,22 +194,38 @@ def tile_attention_pa_kernel(tc, x, freqs_cos, freqs_sin, wq, wk, wv, out_0, out
             nc.vector.tensor_tensor(
                 out=out[:, cols].rearrange("p (h j e) -> p h j e", j=PAIRS, e=2),
                 in0=sums[chunk, i][:, cols].rearrange("p (h j e) -> p h j e", j=PAIRS, e=2)[:, :, :, ::-1],
-                in1=sin_pairs[:, i, :].rearrange("p (j e) -> p j e", e=2).unsqueeze(1).broadcast_to([P, h1 - h0, PAIRS, 2]),
+                in1=trig[i][1][:, :, 0, :].rearrange("p e j -> p j e").unsqueeze(1).broadcast_to([P, h1 - h0, PAIRS, 2]),
                 op=MULT,
             )
 
-        rounds = [[(0, i)] for i in range(3)] + [[(0, i), (0, i + 1)] for i in range(3, 9, 2)]
-        rounds += [[(0, 9 + m), (1, m)] for m in range(2)]
-        rounds += [[(0, 9 + m), (1, m), (2, m - 2)] for m in range(2, 7)]
-        rounds += [[(1, 7 + m), (2, 5 + 2 * m), (2, 6 + 2 * m)] for m in range(2)]
-        rounds += [[(1, i), (2, i)] for i in range(9, TILES - TAIL_TILES)]
-        rounds += [[(c, i) for i in range(TILES - TAIL_TILES, TILES) for c in (1, 2)]]
+        rounds = [[(0, i), (0, i + 1)] for i in range(0, 8, 2)]
+        rounds += [[(0, 8 + m), (1, m)] for m in range(3)]
+        rounds += [[(0, 8 + m), (1, m), (2, m - 3)] for m in range(3, 8)]
+        rounds += [[(1, 8 + m), (2, 5 + 2 * m), (2, 6 + 2 * m)] for m in range(3)]
+        rounds += [[(1, i), (2, i)] for i in range(11, TILES - 2)]
+        rounds += [[(1, TILES - 2)], [(2, TILES - 2), (1, TILES - 1), (2, TILES - 1)]]
+        tensor_units = [(0,4),(0, 6),(0, 8), (0, 9), (1, 7), (1, 10), (1, 13)]
+        def turn_and_add(by_cos, by_sin):
+            bank = psum.tile([P, N], F32, name="turned")
+            for c in range(0, N, P):
+                block = slice(c, c + P)
+                nc.tensor.matmul(out=bank[:, block], lhsT=by_cos[:, block], rhs=ident[:], start=True, stop=False, is_transpose=True)
+                nc.tensor.matmul(out=bank[:, block], lhsT=by_sin[:, block], rhs=ident[:], start=False, stop=True, is_transpose=True)
+            nc.scalar.copy(out=by_sin[:], in_=bank[:])
+
+        def turn_back(chunk, i, by_cos, by_sin):
+            bank = psum.tile([P, N], F32, name="turned")
+            for c in range(0, N, P):
+                nc.tensor.transpose(bank[:, c : c + P], by_sin[:, c : c + P], ident[:])
+            nc.scalar.copy(out=by_cos[:], in_=bank[:])
+            nc.sync.dma_start(out=q_hbm[:, i, chunk * N : (chunk + 1) * N], in_=by_cos[:])
+
         order = [unit for units in rounds for unit in units]
         width = {0: N, 1: N, 2: NKV}
         round_cols = [sum(width[chunk] for chunk, i in units) for units in rounds] + [0]
-        w_due = {5: 1, 7: 2}
-        x_due = [[2], [3]] + [[i, i + 1] for i in range(4, TILES, 2)] + [[]] * len(rounds)
-
+        w_due = {3: 1, 6: 2}
+        x_due = x_groups[3:] + [[]] * len(rounds)
+        locks = [bool(x_due[r]) or r in w_due for r in range(len(rounds) + 1)]
         split = HEAD_VECTOR_COLS
         group_w(nc.vector.tensor_copy, 0, 0, w_rows[0, 0, 0], 0, split)
         group_w(nc.scalar.copy, 0, 0, w_rows[0, 0, 0][:, :, split:], split, N)
@@ -230,31 +234,38 @@ def tile_attention_pa_kernel(tc, x, freqs_cos, freqs_sin, wq, wk, wv, out_0, out
         quantize_w(0, 0, 1)
         group_w(nc.vector.tensor_copy, 0, 1, w_rows[0, 1, 0], 0, split)
         group_w(nc.scalar.copy, 0, 1, w_rows[0, 1, 0][:, :, split:], split, N)
-        negate_sin(sin_early)
-        quantize_x(0, 1)
+        quantize_x([0])
         quantize_w(0, 1, 2)
         ready_chunks = {0}
-        pair_trig(0, 2)
         transpose_x(1)
         group_x(1)
-        quantize_x(1, 1)
-        project(0, 0)
         transpose_x(2)
         group_x(2)
+        quantize_x([1])
+        negate_sin(sin_all)
+        quantize_x([2])
+        project(0, 0)
+        project(0, 1)
+        transpose_x(3)
+        group_x(3)
+        transpose_x(4)
+        group_x(4)
 
-        piece_rounds = range(3, 8)
+        piece_rounds = range(1, 7)
         pieces = {}
         for n in range(2 * PIECES):
             r = piece_rounds[min(n // 3, len(piece_rounds) - 1)]
             pieces.setdefault(r, []).append((1 + n // PIECES, n % PIECES))
 
-        projected = 1
+        waiting = []
+        turned_sum = []
+        projected = 2
         consumed = 0
         for r, units in enumerate(rounds):
             fresh = []
-            while projected < min(len(order), consumed + ACC_BANKS):
+            while projected < min(len(order), consumed + (len(units) + 1 if x_due[r + 1] else ACC_BANKS)):
                 chunk, i = order[projected]
-                if chunk not in ready_chunks or i not in quantized:
+                if chunk not in ready_chunks or i not in x_mx:
                     break
                 project(chunk, i)
                 fresh.append((chunk, i))
@@ -262,8 +273,6 @@ def tile_attention_pa_kernel(tc, x, freqs_cos, freqs_sin, wq, wk, wv, out_0, out
             ahead = x_due[r + 1]
             for i in ahead:
                 transpose_x(i)
-            if x_due[r]:
-                pair_trig(x_due[r][0], len(x_due[r]))
             for chunk, n in pieces.get(r, []):
                 g, c0 = divmod(n * PIECE, N)
                 if chunk == 2:
@@ -274,44 +283,55 @@ def tile_attention_pa_kernel(tc, x, freqs_cos, freqs_sin, wq, wk, wv, out_0, out
                     store_v(i)
             for i in ahead:
                 group_x(i)
+            if turned_sum:
+                turn_back(*turned_sum.pop())
+            if waiting and r >= FIRST_TENSOR_ADD_ROUND:
+                job = waiting.pop(0)
+                turn_and_add(job[2], job[3])
+                turned_sum.append(job)
 
-            total = round_cols[r]
-            last = r == len(rounds) - 1
-            if last:
-                rot = keep.tile([P, total], F32, name="rot_tail")
-                by_sin = keep.tile([P, total], F32, name="by_sin_tail")
+            shared = [unit for unit in units if unit not in tensor_units]
+            total = sum(width[chunk] for chunk, i in shared)
+            rot = flow.tile([P, ROUND_COLS], F32, name="rot", bufs=6)
+            by_sin = flow.tile([P, ROUND_COLS], F32, name="by_sin", bufs=4)
+            if r == len(rounds) - 1:
                 cut = total
+            elif locks[r + 1]:
+                cut = max(0, VECTOR_ADD_COLS + total - round_cols[r + 1])
             else:
-                rot = flow.tile([P, ROUND_COLS], F32, name="rot", bufs=7)
-                by_sin = flow.tile([P, ROUND_COLS], F32, name="by_sin", bufs=4)
-                cut = max(0, VECTOR_ADD_COLS + total - round_cols[r + 1]) if x_due[r + 1] else 0
+                cut = 0
             cols = []
             for chunk, i in units:
+                heads = width[chunk] // HD
+                if (chunk, i) in tensor_units:
+                    own_cos = keep.tile([P, N], F32, name="own_cos%d_%d" % (chunk, i))
+                    own_sin = keep.tile([P, N], F32, name="own_sin%d_%d" % (chunk, i))
+                    times_cos(chunk, i, own_cos[:])
+                    times_sin(chunk, i, own_sin[:], 0, heads)
+                    waiting.append((chunk, i, own_cos, own_sin))
+                    continue
                 start = cols[-1].stop if cols else 0
                 cols.append(slice(start, start + width[chunk]))
-                heads = width[chunk] // HD
-                held_back = 1 if x_due[r] and (chunk, i) == units[-1] else 0
+                held_back = 1 if locks[r] and (chunk, i) == units[-1] else 0
                 times_cos(chunk, i, rot[:, cols[-1]])
                 times_sin(chunk, i, by_sin[:, cols[-1]], 0, heads - held_back)
             consumed += len(units)
 
-            if x_due[r]:
-                quantize_x(x_due[r][0], len(x_due[r]))
             if r in w_due:
                 quantize_w(w_due[r], 0, PASSES)
                 ready_chunks.add(w_due[r])
-            if r == 2:
-                negate_sin(sin_late)
+            if x_due[r]:
+                quantize_x(x_due[r])
             for c in cols:
                 if c.start < cut:
                     mine = slice(c.start, min(c.stop, cut))
                     nc.vector.tensor_tensor(out=rot[:, mine], in0=rot[:, mine], in1=by_sin[:, mine], op=ADD)
-            if x_due[r]:
+            if locks[r]:
                 times_sin(chunk, i, by_sin[:, cols[-1]], heads - 1, heads)
             if cut < total:
                 nc.gpsimd.tensor_tensor(out=rot[:, cut:total], in0=rot[:, cut:total], in1=by_sin[:, cut:total], op=ADD)
 
-            for (chunk, i), c in zip(units, cols):
+            for (chunk, i), c in zip(shared, cols):
                 if chunk < 2:
                     nc.sync.dma_start(out=q_hbm[:, i, chunk * N : (chunk + 1) * N], in_=rot[:, c])
                 else:

from contextlib import ExitStack

import concourse.mybir as mybir
from concourse.masks import make_identity

T, DIM = 2048, 1024
NQ, NKV, HD = 1024, 256, 128
FLOPS = 2 * T * DIM * (NQ + 2 * NKV)

F32 = mybir.dt.float32
BF16 = mybir.dt.bfloat16
U32 = mybir.dt.uint32
U8 = mybir.dt.uint8
E5M2X4 = mybir.dt.float8_e5m2_x4
E4M3X4 = mybir.dt.float8_e4m3fn_x4
MULT = mybir.AluOpType.mult
ADD = mybir.AluOpType.add

P = 128
PACK = 4
K_PASS = P * PACK
PASSES = DIM // K_PASS
TILES = T // P
N = 512
PAIRS = HD // 2
ROT = NQ + NKV
ACC_BANKS = 6
ROUND_COLS = 2 * N + NKV
FIRST_TENSOR_ADD_ROUND = 5
EARLY_TILES = 6
HEAD_VECTOR_COLS = 352
VECTOR_ADD_COLS = 384
PIECE = 128
PIECES = PASSES * N // PIECE


def tile_attention_pa_kernel(tc, x, freqs_cos, freqs_sin, wq, wk, wv, out_0, out_1, out_2):
    nc = tc.nc
    x_hbm = x.rearrange("(p i) k -> p i k", i=TILES)
    cos_hbm = freqs_cos.rearrange("(p i) j -> p i j", i=TILES)
    sin_hbm = freqs_sin.rearrange("(p i) j -> p i j", i=TILES)
    q_hbm = out_0.rearrange("(p i) h d -> p i (h d)", i=TILES)
    k_hbm = out_1.rearrange("(p i) h d -> p i (h d)", i=TILES)
    v_hbm = out_2.rearrange("(p i) h d -> p i (h d)", i=TILES)
    wq_hbm = wq.rearrange("(g p t) n -> p g t n", g=PASSES, t=PACK)
    wk_hbm = wk.rearrange("(g p t) n -> p g t n", g=PASSES, t=PACK)
    wv_hbm = wv.rearrange("(g p t) n -> p g t n", g=PASSES, t=PACK)

    with ExitStack() as ctx:
        keep = ctx.enter_context(tc.tile_pool(name="keep", bufs=1))
        flow = ctx.enter_context(tc.tile_pool(name="flow", bufs=3))
        psum = ctx.enter_context(tc.psum_pool(name="psum", bufs=2))
        ctx.enter_context(tc.manual_schedule())

        ident = keep.tile([P, P], F32, name="ident")
        make_identity(nc, ident[:])

        x_rows = {}
        w_rows = {}
        trig = {}

        def load_x(first, count):
            rows = keep.tile([P, count, DIM], BF16, name="x_rows%d" % first)
            nc.sync.dma_start(out=rows[:], in_=x_hbm[:, first : first + count, :])
            for i in range(count):
                x_rows[first + i] = rows[:, i, :]

        def load_wq(chunk, g):
            rows = keep.tile([P, PACK, N], BF16, name="wq_rows%d_%d" % (chunk, g))
            nc.sync.dma_start(out=rows[:], in_=wq_hbm[:, g, :, chunk * N : (chunk + 1) * N])
            for c in range(0, N, PIECE):
                w_rows[chunk, g, c] = rows[:, :, c:]

        def load_wkv(w_hbm, col0):
            rows = keep.tile([P, PASSES, PACK, NKV], BF16, name="wkv_rows%d" % col0)
            nc.sync.dma_start(out=rows[:], in_=w_hbm)
            for g in range(PASSES):
                for c in range(0, NKV, PIECE):
                    w_rows[2, g, col0 + c] = rows[:, g, :, c:]

        def load_trig(first, count):
            cos = keep.tile([P, count, PAIRS], BF16, name="cos%d" % first)
            sin = keep.tile([P, 2, count, PAIRS], BF16, name="sin%d" % first)
            nc.sync.dma_start(out=cos[:], in_=cos_hbm[:, first : first + count, :])
            nc.sync.dma_start(out=sin[:, 1, :, :], in_=sin_hbm[:, first : first + count, :])
            for i in range(count):
                trig[first + i] = (cos[:, i:, :], sin[:, :, i:, :])
            return sin

        load_wq(0, 0)
        load_x(0, 1)
        load_wq(0, 1)
        load_x(1, 1)
        load_x(2, 1)
        sin_all = load_trig(0, TILES)
        load_x(3, 1)
        load_x(4, 1)
        load_x(5, 2)
        load_wq(1, 0)
        load_x(7, 2)
        load_wq(1, 1)
        load_x(9, 2)
        load_wkv(wk_hbm, 0)
        load_x(11, 2)
        load_wkv(wv_hbm, NKV)
        load_x(13, 3)

        w_grouped = [keep.tile([P, PASSES, N, PACK], BF16, name="w_grouped%d" % c, align_bytes=64) for c in range(3)]
        w_codes = [keep.tile([P, PASSES, N], U32, name="w_codes%d" % c, align_bytes=64) for c in range(3)]
        w_scales = [keep.tile([P, PASSES, N], U8, name="w_scales%d" % c, align_bytes=64) for c in range(3)]
        x_groups = [[0], [1], [2]] + [[i, i + 1] for i in range(3, TILES - 1, 2)] + [[TILES - 1]]
        x_group_of = {i: group for group in x_groups for i in group}

        def group_w(copy, chunk, g, src, c0, c1):
            copy(
                out=w_grouped[chunk][:, g, c0:c1, :].rearrange("p (c i) t -> p c t i", i=4),
                in_=src[:, :, 0 : c1 - c0].rearrange("p t (c i) -> p c t i", i=4),
            )

        def quantize_w(chunk, g0, g1):
            nc.vector.quantize_mx(
                out=w_codes[chunk][:, g0:g1, :].rearrange("p g n -> p (g n)").bitcast(E4M3X4),
                scales=w_scales[chunk][:, g0:g1, :].rearrange("p g n -> p (g n)"),
                in_=w_grouped[chunk][:, g0:g1, :, :].rearrange("p g n t -> p (g n t)"),
            )

        x_mx = {}
        x_turned = {}
        x_grouped = {}

        def transpose_x(i):
            words = x_rows[i].bitcast(F32)
            turned = psum.tile([P, PASSES, 2, P], F32, name="turned")
            for g in range(PASSES):
                for u in range(2):
                    nc.tensor.transpose(turned[:, g, u, :], words[:, 2 * P * g + u : 2 * P * (g + 1) : 2], ident[:])
            x_turned[i] = turned

        def group_x(i):
            group = x_group_of[i]
            if i == group[0]:
                x_grouped[i] = flow.tile([P, len(group), PASSES * P * PACK], BF16, name="grouped", align_bytes=64)
            nc.scalar.copy(
                out=x_grouped[group[0]][:, i - group[0], :].bitcast(F32).rearrange("p (g r u) -> p g r u", g=PASSES, u=2),
                in_=x_turned[i][:].rearrange("p g u r -> p g r u"),
            )

        def quantize_x(group):
            codes = keep.tile([P, len(group), PASSES * P], U32, name="x_codes%d" % group[0], align_bytes=64)
            scales = keep.tile([P, len(group), PASSES * P], U8, name="x_scales%d" % group[0], align_bytes=64)
            nc.vector.quantize_mx(
                out=codes[:].rearrange("p i n -> p (i n)").bitcast(E5M2X4),
                scales=scales[:].rearrange("p i n -> p (i n)"),
                in_=x_grouped[group[0]][:].rearrange("p i n -> p (i n)"),
            )
            for i in group:
                x_mx[i] = (codes[:, i - group[0], :], scales[:, i - group[0], :])

        def negate_sin(sin):
            nc.vector.tensor_scalar_mul(sin[:, 0, :, :], sin[:, 1, :, :], -1.0)

        sums = {}

        def project(chunk, i):
            acc = psum.tile([P, N], F32, name="acc", bufs=ACC_BANKS)
            for g in range(PASSES):
                nc.tensor.matmul_mx(
                    out=acc[:],
                    lhsT=x_mx[i][0][:, g * P : (g + 1) * P].bitcast(E5M2X4),
                    lhsT_scale=x_mx[i][1][:, g * P : (g + 1) * P],
                    rhs=w_codes[chunk][:, g, :].bitcast(E4M3X4),
                    rhs_scale=w_scales[chunk][:, g, :],
                    start=(g == 0),
                    stop=(g == PASSES - 1),
                )
            sums[chunk, i] = acc

        def store_v(i):
            v_sb = flow.tile([P, NKV], F32, name="v_sb", bufs=4)
            nc.scalar.copy(out=v_sb[:], in_=sums[2, i][:, NKV:])
            nc.sync.dma_start(out=v_hbm[:, i, :], in_=v_sb[:])

        def times_cos(chunk, i, out):
            heads = out.shape[1] // HD
            nc.vector.tensor_tensor(
                out=out.rearrange("p (h j e) -> p h j e", j=PAIRS, e=2),
                in0=sums[chunk, i][:, : heads * HD].rearrange("p (h j e) -> p h j e", j=PAIRS, e=2),
                in1=trig[i][0][:, 0, :].unsqueeze(1).unsqueeze(3).broadcast_to([P, heads, PAIRS, 2]),
                op=MULT,
            )

        def times_sin(chunk, i, out, h0, h1):
            cols = slice(h0 * HD, h1 * HD)
            nc.vector.tensor_tensor(
                out=out[:, cols].rearrange("p (h j e) -> p h j e", j=PAIRS, e=2),
                in0=sums[chunk, i][:, cols].rearrange("p (h j e) -> p h j e", j=PAIRS, e=2)[:, :, :, ::-1],
                in1=trig[i][1][:, :, 0, :].rearrange("p e j -> p j e").unsqueeze(1).broadcast_to([P, h1 - h0, PAIRS, 2]),
                op=MULT,
            )

        rounds = [[(0, i), (0, i + 1)] for i in range(0, 8, 2)]
        rounds += [[(0, 8 + m), (1, m)] for m in range(3)]
        rounds += [[(0, 8 + m), (1, m), (2, m - 3)] for m in range(3, 8)]
        rounds += [[(1, 8 + m), (2, 5 + 2 * m), (2, 6 + 2 * m)] for m in range(3)]
        rounds += [[(1, i), (2, i)] for i in range(11, TILES - 2)]
        rounds += [[(1, TILES - 2)], [(2, TILES - 2), (1, TILES - 1), (2, TILES - 1)]]
        tensor_units = [(0,4),(0, 6),(0, 8), (0, 9), (1, 7), (1, 10), (1, 13)]
        def turn_and_add(by_cos, by_sin):
            bank = psum.tile([P, N], F32, name="turned")
            for c in range(0, N, P):
                block = slice(c, c + P)
                nc.tensor.matmul(out=bank[:, block], lhsT=by_cos[:, block], rhs=ident[:], start=True, stop=False, is_transpose=True)
                nc.tensor.matmul(out=bank[:, block], lhsT=by_sin[:, block], rhs=ident[:], start=False, stop=True, is_transpose=True)
            nc.scalar.copy(out=by_sin[:], in_=bank[:])

        def turn_back(chunk, i, by_cos, by_sin):
            bank = psum.tile([P, N], F32, name="turned")
            for c in range(0, N, P):
                nc.tensor.transpose(bank[:, c : c + P], by_sin[:, c : c + P], ident[:])
            nc.scalar.copy(out=by_cos[:], in_=bank[:])
            nc.sync.dma_start(out=q_hbm[:, i, chunk * N : (chunk + 1) * N], in_=by_cos[:])

        order = [unit for units in rounds for unit in units]
        width = {0: N, 1: N, 2: NKV}
        round_cols = [sum(width[chunk] for chunk, i in units) for units in rounds] + [0]
        w_due = {3: 1, 6: 2}
        x_due = x_groups[3:] + [[]] * len(rounds)
        locks = [bool(x_due[r]) or r in w_due for r in range(len(rounds) + 1)]
        split = HEAD_VECTOR_COLS
        group_w(nc.vector.tensor_copy, 0, 0, w_rows[0, 0, 0], 0, split)
        group_w(nc.scalar.copy, 0, 0, w_rows[0, 0, 0][:, :, split:], split, N)
        transpose_x(0)
        group_x(0)
        quantize_w(0, 0, 1)
        group_w(nc.vector.tensor_copy, 0, 1, w_rows[0, 1, 0], 0, split)
        group_w(nc.scalar.copy, 0, 1, w_rows[0, 1, 0][:, :, split:], split, N)
        quantize_x([0])
        quantize_w(0, 1, 2)
        ready_chunks = {0}
        transpose_x(1)
        group_x(1)
        transpose_x(2)
        group_x(2)
        quantize_x([1])
        negate_sin(sin_all)
        quantize_x([2])
        project(0, 0)
        project(0, 1)
        transpose_x(3)
        group_x(3)
        transpose_x(4)
        group_x(4)

        piece_rounds = range(1, 7)
        pieces = {}
        for n in range(2 * PIECES):
            r = piece_rounds[min(n // 3, len(piece_rounds) - 1)]
            pieces.setdefault(r, []).append((1 + n // PIECES, n % PIECES))

        waiting = []
        turned_sum = []
        projected = 2
        consumed = 0
        for r, units in enumerate(rounds):
            fresh = []
            while projected < min(len(order), consumed + (len(units) + 1 if x_due[r + 1] else ACC_BANKS)):
                chunk, i = order[projected]
                if chunk not in ready_chunks or i not in x_mx:
                    break
                project(chunk, i)
                fresh.append((chunk, i))
                projected += 1
            ahead = x_due[r + 1]
            for i in ahead:
                transpose_x(i)
            for chunk, n in pieces.get(r, []):
                g, c0 = divmod(n * PIECE, N)
                if chunk == 2:
                    g, c0 = (n // 2) % 2, (n // 4) * NKV + (n % 2) * PIECE
                group_w(nc.scalar.copy, chunk, g, w_rows[chunk, g, c0], c0, c0 + PIECE)
            for chunk, i in fresh:
                if chunk == 2:
                    store_v(i)
            for i in ahead:
                group_x(i)
            if turned_sum:
                turn_back(*turned_sum.pop())
            if waiting and r >= FIRST_TENSOR_ADD_ROUND:
                job = waiting.pop(0)
                turn_and_add(job[2], job[3])
                turned_sum.append(job)

            shared = [unit for unit in units if unit not in tensor_units]
            total = sum(width[chunk] for chunk, i in shared)
            rot = flow.tile([P, ROUND_COLS], F32, name="rot", bufs=6)
            by_sin = flow.tile([P, ROUND_COLS], F32, name="by_sin", bufs=4)
            if r == len(rounds) - 1:
                cut = total
            elif locks[r + 1]:
                cut = max(0, VECTOR_ADD_COLS + total - round_cols[r + 1])
            else:
                cut = 0
            cols = []
            for chunk, i in units:
                heads = width[chunk] // HD
                if (chunk, i) in tensor_units:
                    own_cos = keep.tile([P, N], F32, name="own_cos%d_%d" % (chunk, i))
                    own_sin = keep.tile([P, N], F32, name="own_sin%d_%d" % (chunk, i))
                    times_cos(chunk, i, own_cos[:])
                    times_sin(chunk, i, own_sin[:], 0, heads)
                    waiting.append((chunk, i, own_cos, own_sin))
                    continue
                start = cols[-1].stop if cols else 0
                cols.append(slice(start, start + width[chunk]))
                held_back = 1 if locks[r] and (chunk, i) == units[-1] else 0
                times_cos(chunk, i, rot[:, cols[-1]])
                times_sin(chunk, i, by_sin[:, cols[-1]], 0, heads - held_back)
            consumed += len(units)

            if r in w_due:
                quantize_w(w_due[r], 0, PASSES)
                ready_chunks.add(w_due[r])
            if x_due[r]:
                quantize_x(x_due[r])
            for c in cols:
                if c.start < cut:
                    mine = slice(c.start, min(c.stop, cut))
                    nc.vector.tensor_tensor(out=rot[:, mine], in0=rot[:, mine], in1=by_sin[:, mine], op=ADD)
            if locks[r]:
                times_sin(chunk, i, by_sin[:, cols[-1]], heads - 1, heads)
            if cut < total:
                nc.gpsimd.tensor_tensor(out=rot[:, cut:total], in0=rot[:, cut:total], in1=by_sin[:, cut:total], op=ADD)

            for (chunk, i), c in zip(shared, cols):
                if chunk < 2:
                    nc.sync.dma_start(out=q_hbm[:, i, chunk * N : (chunk + 1) * N], in_=rot[:, c])
                else:
                    nc.sync.dma_start(out=k_hbm[:, i, :], in_=rot[:, c])
